import numpy as np
import ml_dtypes


def mxq(x, axis, fmt="e4m3"):
    dtype, down = {"e4m3": (ml_dtypes.float8_e4m3fn, 7), "e5m2": (ml_dtypes.float8_e5m2, 14)}[fmt]
    v = np.moveaxis(np.asarray(x, np.float32).astype(ml_dtypes.bfloat16).astype(np.float64), axis, -1)
    blocks = v.reshape(v.shape[:-1] + (-1, 32))
    amax = np.abs(blocks).max(-1, keepdims=True)
    byte = np.maximum(np.where(amax > 0, np.frexp(amax)[1] - 1 + 127, 0) - down, 1)
    scale = np.exp2(byte - 127.0)
    codes = (blocks / scale).astype(np.float32).astype(dtype).astype(np.float64)
    return np.moveaxis((codes * scale).reshape(v.shape), -1, axis)


WIDE = False


def mx_kscale(k):
    if not WIDE:
        return np.ones(k)
    levels = np.array([10, -10, 5, -5, 0])
    a = np.random.permutation(np.resize(levels, k // 512 * 4)).reshape(k // 512, 4)
    idx = np.arange(k)
    return np.exp2(a[idx // 512, idx % 128 // 32])


BF16 = ml_dtypes.bfloat16


def bf(x):
    return np.asarray(x, np.float32).astype(BF16)


def f64(x):
    return np.asarray(x).astype(np.float64)


B, DI, DH = 4096, 512, 512
LR = 0.1
LN_EPS = 1e-5


def softplus(v):
    return np.maximum(v, 0.0) + np.log(1.0 + np.exp(-np.abs(v)))


def layernorm(h, gamma, beta):
    mu = h.mean(axis=-1, keepdims=True)
    var = ((h - mu) ** 2).mean(axis=-1, keepdims=True)
    return (h - mu) / np.sqrt(var + LN_EPS) * gamma + beta


def setup_inputs():
    s = mx_kscale(DI)
    w = s / s.min()
    return {"hidden": bf(np.random.standard_normal((B, DH))),
            "error": bf(1.2 * np.random.standard_normal((B, DI)) * w),
            "Wg": bf(np.random.standard_normal((DI, DH)) / np.sqrt(DH) / w[:, None]),
            "bg": bf(0.3 * np.random.standard_normal(DI) / w),
            "log_precision": bf(0.5 + 0.5 * np.random.standard_normal(DI)),
            "gamma": bf(1.0 + 0.1 * np.random.standard_normal(DH)),
            "beta": bf(0.1 * np.random.standard_normal(DH))}


def reference(hidden, error, Wg, bg, log_precision, gamma, beta):
    wg = f64(Wg)
    precision = softplus(f64(log_precision))
    p2 = precision * precision
    grad = -2.0 * (mxq(f64(error) * p2, 1, "e4m3") @ mxq(wg, 0, "e4m3"))
    hidden_new = layernorm(f64(hidden) - LR * grad, f64(gamma), f64(beta))
    prediction = (mxq(hidden_new, 1, "e4m3") @ mxq(wg.T, 0, "e4m3")) + f64(bg)
    return hidden_new, prediction

@@ -1,0 +1,277 @@
+from contextlib import ExitStack
+
+import concourse.mybir as mybir
+from concourse.masks import make_identity
+
+F32 = mybir.dt.float32
+BF16 = mybir.dt.bfloat16
+U32 = mybir.dt.uint32
+U8 = mybir.dt.uint8
+FP8X4 = mybir.dt.float8_e4m3fn_x4
+ALU = mybir.AluOpType
+ACT = mybir.ActivationFunctionType
+
+P = 128
+B = 4096
+D = 512
+QUADS = B // (4 * P)
+PAIRS = B // (2 * P)
+FLOPS = 2 * 2 * B * D * D
+
+E_ON_VECTOR = ()
+
+
+def tile_predictivecodinglayer_pb_t_kernel(
+    tc, hidden, error, Wg, bg, log_precision, gamma, beta, out_0, out_1
+):
+    nc = tc.nc
+    with ExitStack() as ctx:
+        consts = ctx.enter_context(tc.tile_pool(name="consts", bufs=1))
+        inputs = ctx.enter_context(tc.tile_pool(name="inputs", bufs=1))
+        work = ctx.enter_context(tc.tile_pool(name="work", bufs=3))
+        small = ctx.enter_context(tc.tile_pool(name="small", bufs=6))
+        psum = ctx.enter_context(tc.psum_pool(name="psum", bufs=2))
+
+        lp = consts.tile([P, 4], BF16, name="lp")
+        nc.sync.dma_start(
+            out=lp[:].rearrange("p (u e) -> p u e", u=2),
+            in_=log_precision.rearrange("(u p e) -> p u e", u=2, e=2),
+        )
+        err = []
+        hid = []
+        w1raw = consts.tile([P, 4, D], BF16, name="w1raw")
+        w2raw = consts.tile([P, 4, D], BF16, name="w2raw")
+        for q in range(QUADS):
+            rows = slice(4 * P * q, 4 * P * (q + 1))
+            err_q = inputs.tile([P, 4 * D], BF16, name="err%d" % q)
+            nc.sync.dma_start(out=err_q[:], in_=error[rows, :].rearrange("(p j) k -> p (j k)", j=4))
+            err.append(err_q)
+            if q == 0:
+                nc.sync.dma_start(
+                    out=w1raw[:].rearrange("p (u e) n -> p u e n", u=2),
+                    in_=Wg.rearrange("(u p e) n -> p u e n", u=2, e=2),
+                )
+            hid_q = inputs.tile([P, 4 * D], BF16, name="hid%d" % q)
+            nc.sync.dma_start(out=hid_q[:], in_=hidden[rows, :].rearrange("(p j) k -> p (j k)", j=4))
+            hid.append(hid_q)
+            if q == 0:
+                nc.sync.dma_start(out=w2raw[:], in_=Wg.rearrange("(c p) k -> p c k", p=P))
+        gam_b = consts.tile([P, D], BF16, name="gam_b")
+        bet_b = consts.tile([P, D], BF16, name="bet_b")
+        bg_b = consts.tile([P, D], BF16, name="bg_b")
+        nc.scalar.dma_start(out=gam_b[:], in_=gamma.partition_broadcast(P))
+        nc.scalar.dma_start(out=bet_b[:], in_=beta.partition_broadcast(P))
+        nc.scalar.dma_start(out=bg_b[:], in_=bg.partition_broadcast(P))
+
+        ident_f = consts.tile([P, P], F32, name="ident_f")
+        make_identity(nc, ident_f[:])
+        ident_b = consts.tile([P, P], BF16, name="ident_b")
+        make_identity(nc, ident_b[:])
+        eps_t = consts.tile([P, 1], F32, name="eps_t")
+        nc.vector.memset(eps_t[:], 1e-5)
+        one_t = consts.tile([P, 1], F32, name="one_t")
+        nc.vector.memset(one_t[:], 1.0)
+
+        absv = consts.tile([P, 4], F32, name="absv")
+        nc.scalar.activation(out=absv[:], in_=lp[:], func=ACT.Abs)
+        expv = consts.tile([P, 4], F32, name="expv")
+        nc.scalar.activation(out=expv[:], in_=absv[:], func=ACT.Exp, scale=-1.0)
+        lnv = consts.tile([P, 4], F32, name="lnv")
+        nc.scalar.activation(out=lnv[:], in_=expv[:], func=ACT.Ln, bias=one_t[:], scale=1.0)
+        spv = consts.tile([P, 4], F32, name="spv")
+        nc.vector.scalar_tensor_tensor(
+            out=spv[:], in0=lp[:], scalar=0.0, in1=lnv[:], op0=ALU.max, op1=ALU.add
+        )
+        p2w = consts.tile([P, 4], F32, name="p2w")
+        nc.vector.tensor_tensor(out=p2w[:], in0=spv[:], in1=spv[:], op=ALU.mult)
+
+        w1grp = consts.tile([P, D, 4], BF16, name="w1grp", align_bytes=64)
+        nc.vector.tensor_copy(out=w1grp[:], in_=w1raw[:].rearrange("p t n -> p n t"))
+        w1codes = consts.tile([P, D], U32, name="w1codes", align_bytes=64)
+        w1sc = consts.tile([P, D], U8, name="w1sc", align_bytes=64)
+        nc.vector.quantize_mx(
+            out=w1codes[:].bitcast(FP8X4), scales=w1sc[:], in_=w1grp[:].rearrange("p n t -> p (n t)")
+        )
+
+        w2grp = consts.tile([P, D, 4], BF16, name="w2grp", align_bytes=64)
+        w2codes = consts.tile([P, D], U32, name="w2codes", align_bytes=64)
+        w2sc = consts.tile([P, D], U8, name="w2sc", align_bytes=64)
+
+        def prepare_w2():
+            for h in range(2):
+                w_t = psum.tile([P, 4, 2 * P], BF16, name="w_t", tag="hT")
+                for t in range(4):
+                    for c2 in range(2):
+                        nc.tensor.transpose(
+                            w_t[:, t, P * c2 : P * (c2 + 1)],
+                            w2raw[:, 2 * h + c2, P * t : P * (t + 1)],
+                            ident_b[:],
+                        )
+                nc.scalar.copy(
+                    out=w2grp[:, 2 * P * h : 2 * P * (h + 1), :], in_=w_t[:].rearrange("p t n -> p n t")
+                )
+            nc.vector.quantize_mx(
+                out=w2codes[:].bitcast(FP8X4), scales=w2sc[:], in_=w2grp[:].rearrange("p n t -> p (n t)")
+            )
+
+        out0_v = out_0.rearrange("(q p j) k -> q p j k", p=P, j=4)
+        out1_v = out_1.rearrange("(q p j) k -> q p j k", p=P, j=4)
+        st = {}
+
+        def stage_a(g):
+            q, j0 = g // 2, 2 * (g % 2)
+            errw = err[q][:].bitcast(F32)
+            xt = psum.tile([P, D], F32, name="xt", tag="xt")
+            for j2 in range(2):
+                for u in range(2):
+                    nc.tensor.transpose(
+                        xt[:, 256 * u + P * j2 : 256 * u + P * (j2 + 1)],
+                        errw[:, 256 * (j0 + j2) + P * u : 256 * (j0 + j2) + P * (u + 1)],
+                        ident_f[:],
+                    )
+            g1 = work.tile([P, 2 * D], BF16, name="g1", tag="g1", align_bytes=64)
+            nc.vector.tensor_tensor(
+                out=g1[:].rearrange("p (r u e) -> p r u e", u=2, e=2),
+                in0=xt[:].bitcast(BF16).rearrange("p (u r e) -> p r u e", u=2, e=2),
+                in1=p2w[:].rearrange("p (u e) -> p u e", u=2).unsqueeze(1).to_broadcast([P, 2 * P, 2, 2]),
+                op=ALU.mult,
+            )
+            st[("g1", g)] = g1
+
+        def stage_b(g):
+            c1 = work.tile([P, 2 * P], U32, name="c1", tag="c1", align_bytes=64)
+            s1 = work.tile([P, 2 * P], U8, name="s1", tag="s1", align_bytes=64)
+            nc.vector.quantize_mx(out=c1[:].bitcast(FP8X4), scales=s1[:], in_=st[("g1", g)][:])
+            for j2 in range(2):
+                cols = slice(P * j2, P * (j2 + 1))
+                g_ps = psum.tile([P, D], F32, name="g_ps", tag="G")
+                nc.tensor.matmul_mx(
+                    out=g_ps[:],
+                    lhsT=c1[:, cols].bitcast(FP8X4),
+                    lhsT_scale=s1[:, cols],
+                    rhs=w1codes[:].bitcast(FP8X4),
+                    rhs_scale=w1sc[:],
+                    start=True,
+                    stop=True,
+                )
+                st[("G", g, j2)] = g_ps
+
+        def stage_c(g):
+            q, j0 = g // 2, 2 * (g % 2)
+            sums = small.tile([P, 2], F32, name="sums", tag="sums")
+            for j2 in range(2):
+                u_t = work.tile([P, D], F32, name="u_t", tag="u", bufs=6)
+                nc.vector.scalar_tensor_tensor(
+                    out=u_t[:],
+                    in0=st[("G", g, j2)][:],
+                    scalar=0.2,
+                    in1=hid[q][:, D * (j0 + j2) : D * (j0 + j2 + 1)],
+                    op0=ALU.mult,
+                    op1=ALU.add,
+                    accum_out=sums[:, j2 : j2 + 1],
+                )
+                st[("u", g, j2)] = u_t
+            st[("sums", g)] = sums
+
+        def stage_d(g):
+            negmean = small.tile([P, 2], F32, name="negmean", tag="negmean")
+            nc.scalar.mul(out=negmean[:], in_=st[("sums", g)][:], mul=-1.0 / D)
+            ssq = small.tile([P, 2], F32, name="ssq", tag="ssq")
+            for j2 in range(2):
+                junk = work.tile([P, D], BF16, name="junk", tag="junk", bufs=2)
+                nc.scalar.activation(
+                    out=junk[:],
+                    in_=st[("u", g, j2)][:],
+                    func=ACT.Square,
+                    bias=negmean[:, j2 : j2 + 1],
+                    scale=1.0,
+                    accum_out=ssq[:, j2 : j2 + 1],
+                )
+            std = small.tile([P, 2], F32, name="std", tag="std")
+            nc.scalar.activation(out=std[:], in_=ssq[:], func=ACT.Sqrt, bias=eps_t[:], scale=1.0 / D)
+            rstd = small.tile([P, 2], F32, name="rstd", tag="rstd")
+            nc.vector.reciprocal(out=rstd[:], in_=std[:])
+            nmr = small.tile([P, 2], F32, name="nmr", tag="nmr")
+            nc.vector.tensor_tensor(out=nmr[:], in0=negmean[:], in1=rstd[:], op=ALU.mult)
+            st[("stats", g)] = (negmean, rstd, nmr)
+
+        def stage_e(g):
+            q, j0 = g // 2, 2 * (g % 2)
+            negmean, rstd, nmr = st[("stats", g)]
+            hn = work.tile([P, 2, D], F32, name="hn", tag="hn", bufs=4)
+            for j2 in range(2):
+                u_t = st[("u", g, j2)]
+                col = slice(j2, j2 + 1)
+                z_t = work.tile([P, D], F32, name="z_t", tag="z", bufs=4)
+                if 2 * g + j2 in E_ON_VECTOR:
+                    nc.vector.scalar_tensor_tensor(
+                        out=z_t[:], in0=u_t[:], scalar=negmean[:, col], in1=gam_b[:], op0=ALU.add, op1=ALU.mult
+                    )
+                    nc.vector.scalar_tensor_tensor(
+                        out=hn[:, j2, :], in0=z_t[:], scalar=rstd[:, col], in1=bet_b[:], op0=ALU.mult, op1=ALU.add
+                    )
+                else:
+                    nc.scalar.activation(
+                        out=z_t[:], in_=u_t[:], func=ACT.Identity, bias=nmr[:, col], scale=rstd[:, col]
+                    )
+                    nc.gpsimd.tensor_tensor(out=z_t[:], in0=z_t[:], in1=gam_b[:], op=ALU.mult)
+                    nc.gpsimd.tensor_tensor(out=hn[:, j2, :], in0=z_t[:], in1=bet_b[:], op=ALU.add)
+            nc.sync.dma_start(out=out0_v[q, :, j0 : j0 + 2, :], in_=hn[:])
+            st[("hn", g)] = hn
+
+        def stage_f(g):
+            hn = st[("hn", g)]
+            g2 = work.tile([P, 2 * D], BF16, name="g2", tag="g2", align_bytes=64)
+            for j2 in range(2):
+                h_t = psum.tile([P, 4, P], F32, name="h_t", tag="hT")
+                for t in range(4):
+                    nc.tensor.transpose(h_t[:, t, :], hn[:, j2, P * t : P * (t + 1)], ident_f[:])
+                nc.scalar.copy(
+                    out=g2[:, D * j2 : D * (j2 + 1)].rearrange("p (r t) -> p r t", t=4),
+                    in_=h_t[:].rearrange("p t r -> p r t"),
+                )
+            st[("g2", g)] = g2
+
+        def stage_q2(g):
+            c2 = work.tile([P, 2 * P], U32, name="c2", tag="c2", align_bytes=64)
+            s2 = work.tile([P, 2 * P], U8, name="s2", tag="s2", align_bytes=64)
+            nc.vector.quantize_mx(out=c2[:].bitcast(FP8X4), scales=s2[:], in_=st[("g2", g)][:])
+            for j2 in range(2):
+                cols = slice(P * j2, P * (j2 + 1))
+                p_ps = psum.tile([P, D], F32, name="p_ps", tag="P")
+                nc.tensor.matmul_mx(
+                    out=p_ps[:],
+                    lhsT=c2[:, cols].bitcast(FP8X4),
+                    lhsT_scale=s2[:, cols],
+                    rhs=w2codes[:].bitcast(FP8X4),
+                    rhs_scale=w2sc[:],
+                    start=True,
+                    stop=True,
+                )
+                st[("P", g, j2)] = p_ps
+
+        def stage_h(g):
+            q, j0 = g // 2, 2 * (g % 2)
+            pred = work.tile([P, 2, D], F32, name="pred", tag="pred", bufs=4)
+            for j2 in range(2):
+                nc.vector.tensor_tensor(out=pred[:, j2, :], in0=st[("P", g, j2)][:], in1=bg_b[:], op=ALU.add)
+            nc.sync.dma_start(out=out1_v[q, :, j0 : j0 + 2, :], in_=pred[:])
+
+        for i in range(PAIRS + 5):
+            if i < PAIRS:
+                stage_a(i)
+            if 0 <= i - 1 < PAIRS:
+                stage_c(i - 1)
+            if i < PAIRS:
+                stage_b(i)
+            if i == 0:
+                prepare_w2()
+            if 0 <= i - 1 < PAIRS:
+                stage_d(i - 1)
+                stage_e(i - 1)
+            if 0 <= i - 3 < PAIRS:
+                stage_f(i - 3)
+            if 0 <= i - 5 < PAIRS:
+                stage_h(i - 5)
+            if 0 <= i - 4 < PAIRS:
+                stage_q2(i - 4)

@@ -18,8 +18,6 @@ QUADS = B // (4 * P)
 PAIRS = B // (2 * P)
 FLOPS = 2 * 2 * B * D * D
 
-E_ON_VECTOR = ()
-
 
 def tile_predictivecodinglayer_pb_t_kernel(
     tc, hidden, error, Wg, bg, log_precision, gamma, beta, out_0, out_1
@@ -56,11 +54,12 @@ def tile_predictivecodinglayer_pb_t_kernel(
             hid.append(hid_q)
             if q == 0:
                 nc.sync.dma_start(out=w2raw[:], in_=Wg.rearrange("(c p) k -> p c k", p=P))
-        gam_b = consts.tile([P, D], BF16, name="gam_b")
-        bet_b = consts.tile([P, D], BF16, name="bet_b")
+        gam_raw = consts.tile([P, 4], BF16, name="gam_raw")
+        bet_raw = consts.tile([P, 4], BF16, name="bet_raw")
+        with nc.allow_non_contiguous_dma(reason="two vectors of 512, one element to a partition, once"):
+            nc.scalar.dma_start(out=gam_raw[:], in_=gamma.rearrange("(t p) -> p t", p=P))
+            nc.scalar.dma_start(out=bet_raw[:], in_=beta.rearrange("(t p) -> p t", p=P))
         bg_b = consts.tile([P, D], BF16, name="bg_b")
-        nc.scalar.dma_start(out=gam_b[:], in_=gamma.partition_broadcast(P))
-        nc.scalar.dma_start(out=bet_b[:], in_=beta.partition_broadcast(P))
         nc.scalar.dma_start(out=bg_b[:], in_=bg.partition_broadcast(P))
 
         ident_f = consts.tile([P, P], F32, name="ident_f")
@@ -84,6 +83,12 @@ def tile_predictivecodinglayer_pb_t_kernel(
         )
         p2w = consts.tile([P, 4], F32, name="p2w")
         nc.vector.tensor_tensor(out=p2w[:], in0=spv[:], in1=spv[:], op=ALU.mult)
+        warm = consts.tile([P, 1], F32, name="warm")
+        nc.scalar.activation(out=warm[:], in_=one_t[:], func=ACT.Abs_reciprocal_sqrt)
+        gam_t = consts.tile([P, 4], F32, name="gam_t")
+        nc.vector.tensor_copy(out=gam_t[:], in_=gam_raw[:])
+        bet_t = consts.tile([P, 4], F32, name="bet_t")
+        nc.vector.tensor_copy(out=bet_t[:], in_=bet_raw[:])
 
         w1grp = consts.tile([P, D, 4], BF16, name="w1grp", align_bytes=64)
         nc.vector.tensor_copy(out=w1grp[:], in_=w1raw[:].rearrange("p t n -> p n t"))
@@ -99,7 +104,7 @@ def tile_predictivecodinglayer_pb_t_kernel(
 
         def prepare_w2():
             for h in range(2):
-                w_t = psum.tile([P, 4, 2 * P], BF16, name="w_t", tag="hT")
+                w_t = psum.tile([P, 4, 2 * P], BF16, name="w_t", tag="zT")
                 for t in range(4):
                     for c2 in range(2):
                         nc.tensor.transpose(
@@ -121,7 +126,7 @@ def tile_predictivecodinglayer_pb_t_kernel(
         def stage_a(g):
             q, j0 = g // 2, 2 * (g % 2)
             errw = err[q][:].bitcast(F32)
-            xt = psum.tile([P, D], F32, name="xt", tag="xt")
+            xt = psum.tile([P, D], F32, name="xt", tag="xt", bufs=1)
             for j2 in range(2):
                 for u in range(2):
                     nc.tensor.transpose(
@@ -187,50 +192,69 @@ def tile_predictivecodinglayer_pb_t_kernel(
                     scale=1.0,
                     accum_out=ssq[:, j2 : j2 + 1],
                 )
-            std = small.tile([P, 2], F32, name="std", tag="std")
-            nc.scalar.activation(out=std[:], in_=ssq[:], func=ACT.Sqrt, bias=eps_t[:], scale=1.0 / D)
             rstd = small.tile([P, 2], F32, name="rstd", tag="rstd")
-            nc.vector.reciprocal(out=rstd[:], in_=std[:])
-            nmr = small.tile([P, 2], F32, name="nmr", tag="nmr")
-            nc.vector.tensor_tensor(out=nmr[:], in0=negmean[:], in1=rstd[:], op=ALU.mult)
-            st[("stats", g)] = (negmean, rstd, nmr)
+            nc.scalar.activation(
+                out=rstd[:], in_=ssq[:], func=ACT.Abs_reciprocal_sqrt, bias=eps_t[:], scale=1.0 / D
+            )
+            st[("stats", g)] = (negmean, rstd)
 
-        def stage_e(g):
-            q, j0 = g // 2, 2 * (g % 2)
-            negmean, rstd, nmr = st[("stats", g)]
-            hn = work.tile([P, 2, D], F32, name="hn", tag="hn", bufs=4)
+        def stage_z(g):
+            negmean, rstd = st[("stats", g)]
             for j2 in range(2):
-                u_t = st[("u", g, j2)]
-                col = slice(j2, j2 + 1)
                 z_t = work.tile([P, D], F32, name="z_t", tag="z", bufs=4)
-                if 2 * g + j2 in E_ON_VECTOR:
-                    nc.vector.scalar_tensor_tensor(
-                        out=z_t[:], in0=u_t[:], scalar=negmean[:, col], in1=gam_b[:], op0=ALU.add, op1=ALU.mult
-                    )
-                    nc.vector.scalar_tensor_tensor(
-                        out=hn[:, j2, :], in0=z_t[:], scalar=rstd[:, col], in1=bet_b[:], op0=ALU.mult, op1=ALU.add
-                    )
-                else:
-                    nc.scalar.activation(
-                        out=z_t[:], in_=u_t[:], func=ACT.Identity, bias=nmr[:, col], scale=rstd[:, col]
-                    )
-                    nc.gpsimd.tensor_tensor(out=z_t[:], in0=z_t[:], in1=gam_b[:], op=ALU.mult)
-                    nc.gpsimd.tensor_tensor(out=hn[:, j2, :], in0=z_t[:], in1=bet_b[:], op=ALU.add)
-            nc.sync.dma_start(out=out0_v[q, :, j0 : j0 + 2, :], in_=hn[:])
-            st[("hn", g)] = hn
-
-        def stage_f(g):
-            hn = st[("hn", g)]
-            g2 = work.tile([P, 2 * D], BF16, name="g2", tag="g2", align_bytes=64)
-            for j2 in range(2):
-                h_t = psum.tile([P, 4, P], F32, name="h_t", tag="hT")
-                for t in range(4):
-                    nc.tensor.transpose(h_t[:, t, :], hn[:, j2, P * t : P * (t + 1)], ident_f[:])
-                nc.scalar.copy(
-                    out=g2[:, D * j2 : D * (j2 + 1)].rearrange("p (r t) -> p r t", t=4),
-                    in_=h_t[:].rearrange("p t r -> p r t"),
+                nc.gpsimd.tensor_scalar(
+                    out=z_t[:],
+                    in0=st[("u", g, j2)][:],
+                    scalar1=negmean[:, j2 : j2 + 1],
+                    scalar2=rstd[:, j2 : j2 + 1],
+                    op0=ALU.add,
+                    op1=ALU.mult,
                 )
+                st[("z", g, j2)] = z_t
+
+        def stage_t(g):
+            hn_t = work.tile([P, 4, 2 * P], F32, name="hn_t", tag="hn_t")
+            for half in range(2):
+                z_ps = psum.tile([P, 2, 2 * P], F32, name="z_ps", tag="zT")
+                for t2 in range(2):
+                    t = 2 * half + t2
+                    for j2 in range(2):
+                        nc.tensor.transpose(
+                            z_ps[:, t2, P * j2 : P * (j2 + 1)], st[("z", g, j2)][:, P * t : P * (t + 1)], ident_f[:]
+                        )
+                for t2 in range(2):
+                    t = 2 * half + t2
+                    nc.scalar.activation(
+                        out=hn_t[:, t, :],
+                        in_=z_ps[:, t2, :],
+                        func=ACT.Identity,
+                        bias=bet_t[:, t : t + 1],
+                        scale=gam_t[:, t : t + 1],
+                    )
+            st[("hn_t", g)] = hn_t
+
+        def stage_r(g):
+            g2 = work.tile([P, 2 * D], BF16, name="g2", tag="g2", align_bytes=64)
+            nc.gpsimd.tensor_scalar(
+                out=g2[:].rearrange("p (r t) -> p r t", t=4),
+                in0=st[("hn_t", g)][:].rearrange("p t r -> p r t"),
+                scalar1=1.0,
+                scalar2=0.0,
+                op0=ALU.mult,
+                op1=ALU.add,
+            )
             st[("g2", g)] = g2
+
+        def stage_o(g):
+            q, j0 = g // 2, 2 * (g % 2)
+            hn_t = st[("hn_t", g)]
+            hn = work.tile([P, 2, D], F32, name="hn", tag="hn")
+            for j2 in range(2):
+                h_ps = psum.tile([P, D], F32, name="h_ps", tag="hB", bufs=1)
+                for t in range(4):
+                    nc.tensor.transpose(h_ps[:, P * t : P * (t + 1)], hn_t[:, t, P * j2 : P * (j2 + 1)], ident_f[:])
+                nc.scalar.copy(out=hn[:, j2, :], in_=h_ps[:])
+            nc.sync.dma_start(out=out0_v[q, :, j0 : j0 + 2, :], in_=hn[:])
 
         def stage_q2(g):
             c2 = work.tile([P, 2 * P], U32, name="c2", tag="c2", align_bytes=64)
@@ -252,26 +276,25 @@ def tile_predictivecodinglayer_pb_t_kernel(
 
         def stage_h(g):
             q, j0 = g // 2, 2 * (g % 2)
-            pred = work.tile([P, 2, D], F32, name="pred", tag="pred", bufs=4)
+            pred = work.tile([P, 2, D], F32, name="pred", tag="pred")
             for j2 in range(2):
                 nc.vector.tensor_tensor(out=pred[:, j2, :], in0=st[("P", g, j2)][:], in1=bg_b[:], op=ALU.add)
             nc.sync.dma_start(out=out1_v[q, :, j0 : j0 + 2, :], in_=pred[:])
 
-        for i in range(PAIRS + 5):
-            if i < PAIRS:
-                stage_a(i)
-            if 0 <= i - 1 < PAIRS:
-                stage_c(i - 1)
-            if i < PAIRS:
-                stage_b(i)
+        def run(stage, g):
+            if 0 <= g < PAIRS:
+                stage(g)
+
+        for i in range(PAIRS + 4):
+            run(stage_a, i)
+            run(stage_c, i - 1)
+            run(stage_b, i)
             if i == 0:
                 prepare_w2()
-            if 0 <= i - 1 < PAIRS:
-                stage_d(i - 1)
-                stage_e(i - 1)
-            if 0 <= i - 3 < PAIRS:
-                stage_f(i - 3)
-            if 0 <= i - 5 < PAIRS:
-                stage_h(i - 5)
-            if 0 <= i - 4 < PAIRS:
-                stage_q2(i - 4)
+            run(stage_h, i - 4)
+            run(stage_q2, i - 3)
+            run(stage_d, i - 1)
+            run(stage_t, i - 2)
+            run(stage_o, i - 3)
+            run(stage_z, i - 1)
+            run(stage_r, i - 2)

@@ -14,9 +14,9 @@ ACT = mybir.ActivationFunctionType
 P = 128
 B = 4096
 D = 512
-QUADS = B // (4 * P)
 PAIRS = B // (2 * P)
 FLOPS = 2 * 2 * B * D * D
+PINNED = True
 
 
 def tile_predictivecodinglayer_pb_t_kernel(
@@ -26,41 +26,47 @@ def tile_predictivecodinglayer_pb_t_kernel(
     with ExitStack() as ctx:
         consts = ctx.enter_context(tc.tile_pool(name="consts", bufs=1))
         inputs = ctx.enter_context(tc.tile_pool(name="inputs", bufs=1))
-        work = ctx.enter_context(tc.tile_pool(name="work", bufs=3))
-        small = ctx.enter_context(tc.tile_pool(name="small", bufs=6))
-        psum = ctx.enter_context(tc.psum_pool(name="psum", bufs=2))
+        work = ctx.enter_context(tc.tile_pool(name="work", bufs=2))
+        small = ctx.enter_context(tc.tile_pool(name="small", bufs=4))
+        psum = ctx.enter_context(tc.psum_pool(name="psum", bufs=1))
+        if PINNED:
+            ctx.enter_context(tc.manual_schedule())
 
+        err_v = error.rearrange("(g p j) k -> g p (j k)", p=P, j=2)
+        hid_v = hidden.rearrange("(g p j) k -> g p (j k)", p=P, j=2)
+        out0_v = out_0.rearrange("(g p j) k -> g p j k", p=P, j=2)
+        out1_v = out_1.rearrange("(g p j) k -> g p j k", p=P, j=2)
         lp = consts.tile([P, 4], BF16, name="lp")
         nc.sync.dma_start(
             out=lp[:].rearrange("p (u e) -> p u e", u=2),
             in_=log_precision.rearrange("(u p e) -> p u e", u=2, e=2),
         )
-        err = []
-        hid = []
         w1raw = consts.tile([P, 4, D], BF16, name="w1raw")
         w2raw = consts.tile([P, 4, D], BF16, name="w2raw")
-        for q in range(QUADS):
-            rows = slice(4 * P * q, 4 * P * (q + 1))
-            err_q = inputs.tile([P, 4 * D], BF16, name="err%d" % q)
-            nc.sync.dma_start(out=err_q[:], in_=error[rows, :].rearrange("(p j) k -> p (j k)", j=4))
-            err.append(err_q)
-            if q == 0:
-                nc.sync.dma_start(
-                    out=w1raw[:].rearrange("p (u e) n -> p u e n", u=2),
-                    in_=Wg.rearrange("(u p e) n -> p u e n", u=2, e=2),
-                )
-            hid_q = inputs.tile([P, 4 * D], BF16, name="hid%d" % q)
-            nc.sync.dma_start(out=hid_q[:], in_=hidden[rows, :].rearrange("(p j) k -> p (j k)", j=4))
-            hid.append(hid_q)
-            if q == 0:
-                nc.sync.dma_start(out=w2raw[:], in_=Wg.rearrange("(c p) k -> p c k", p=P))
         gam_raw = consts.tile([P, 4], BF16, name="gam_raw")
         bet_raw = consts.tile([P, 4], BF16, name="bet_raw")
-        with nc.allow_non_contiguous_dma(reason="two vectors of 512, one element to a partition, once"):
-            nc.scalar.dma_start(out=gam_raw[:], in_=gamma.rearrange("(t p) -> p t", p=P))
-            nc.scalar.dma_start(out=bet_raw[:], in_=beta.rearrange("(t p) -> p t", p=P))
         bg_b = consts.tile([P, D], BF16, name="bg_b")
-        nc.scalar.dma_start(out=bg_b[:], in_=bg.partition_broadcast(P))
+        nc.sync.dma_start(
+            out=w1raw[:].rearrange("p (u e) n -> p u e n", u=2),
+            in_=Wg.rearrange("(u p e) n -> p u e n", u=2, e=2),
+        )
+        err = []
+        hid = []
+        for g in range(PAIRS):
+            err_g = inputs.tile([P, 2 * D], BF16, name="err%d" % g)
+            nc.sync.dma_start(out=err_g[:], in_=err_v[g])
+            err.append(err_g)
+            hid_g = inputs.tile([P, 2 * D], BF16, name="hid%d" % g)
+            nc.sync.dma_start(out=hid_g[:], in_=hid_v[g])
+            hid.append(hid_g)
+            if g == 0:
+                nc.sync.dma_start(out=w2raw[:], in_=Wg.rearrange("(c p) k -> p c k", p=P))
+            if g == 1:
+                with nc.allow_non_contiguous_dma(reason="two vectors of 512, one element to a partition, once"):
+                    nc.sync.dma_start(out=gam_raw[:], in_=gamma.rearrange("(t p) -> p t", p=P))
+                    nc.sync.dma_start(out=bet_raw[:], in_=beta.rearrange("(t p) -> p t", p=P))
+            if g == 2:
+                nc.sync.dma_start(out=bg_b[:], in_=bg.partition_broadcast(P))
 
         ident_f = consts.tile([P, P], F32, name="ident_f")
         make_identity(nc, ident_f[:])
@@ -71,169 +77,177 @@ def tile_predictivecodinglayer_pb_t_kernel(
         one_t = consts.tile([P, 1], F32, name="one_t")
         nc.vector.memset(one_t[:], 1.0)
 
+        w1grp = consts.tile([P, D, 4], BF16, name="w1grp", align_bytes=64)
+        nc.vector.tensor_copy(out=w1grp[:], in_=w1raw[:].rearrange("p t n -> p n t"))
+
         absv = consts.tile([P, 4], F32, name="absv")
         nc.scalar.activation(out=absv[:], in_=lp[:], func=ACT.Abs)
         expv = consts.tile([P, 4], F32, name="expv")
         nc.scalar.activation(out=expv[:], in_=absv[:], func=ACT.Exp, scale=-1.0)
         lnv = consts.tile([P, 4], F32, name="lnv")
         nc.scalar.activation(out=lnv[:], in_=expv[:], func=ACT.Ln, bias=one_t[:], scale=1.0)
+        warm = consts.tile([P, 1], F32, name="warm")
+        nc.scalar.activation(out=warm[:], in_=one_t[:], func=ACT.Abs_reciprocal_sqrt)
         spv = consts.tile([P, 4], F32, name="spv")
         nc.vector.scalar_tensor_tensor(
             out=spv[:], in0=lp[:], scalar=0.0, in1=lnv[:], op0=ALU.max, op1=ALU.add
         )
         p2w = consts.tile([P, 4], F32, name="p2w")
         nc.vector.tensor_tensor(out=p2w[:], in0=spv[:], in1=spv[:], op=ALU.mult)
-        warm = consts.tile([P, 1], F32, name="warm")
-        nc.scalar.activation(out=warm[:], in_=one_t[:], func=ACT.Abs_reciprocal_sqrt)
-        gam_t = consts.tile([P, 4], F32, name="gam_t")
-        nc.vector.tensor_copy(out=gam_t[:], in_=gam_raw[:])
-        bet_t = consts.tile([P, 4], F32, name="bet_t")
-        nc.vector.tensor_copy(out=bet_t[:], in_=bet_raw[:])
 
-        w1grp = consts.tile([P, D, 4], BF16, name="w1grp", align_bytes=64)
-        nc.vector.tensor_copy(out=w1grp[:], in_=w1raw[:].rearrange("p t n -> p n t"))
         w1codes = consts.tile([P, D], U32, name="w1codes", align_bytes=64)
         w1sc = consts.tile([P, D], U8, name="w1sc", align_bytes=64)
-        nc.vector.quantize_mx(
-            out=w1codes[:].bitcast(FP8X4), scales=w1sc[:], in_=w1grp[:].rearrange("p n t -> p (n t)")
-        )
 
         w2grp = consts.tile([P, D, 4], BF16, name="w2grp", align_bytes=64)
         w2codes = consts.tile([P, D], U32, name="w2codes", align_bytes=64)
         w2sc = consts.tile([P, D], U8, name="w2sc", align_bytes=64)
+        gam_t = consts.tile([P, 4], F32, name="gam_t")
+        bet_t = consts.tile([P, 4], F32, name="bet_t")
+        st = {}
 
-        def prepare_w2():
-            for h in range(2):
-                w_t = psum.tile([P, 4, 2 * P], BF16, name="w_t", tag="zT")
-                for t in range(4):
-                    for c2 in range(2):
-                        nc.tensor.transpose(
-                            w_t[:, t, P * c2 : P * (c2 + 1)],
-                            w2raw[:, 2 * h + c2, P * t : P * (t + 1)],
-                            ident_b[:],
-                        )
-                nc.scalar.copy(
-                    out=w2grp[:, 2 * P * h : 2 * P * (h + 1), :], in_=w_t[:].rearrange("p t n -> p n t")
-                )
+        def w2_transposes(half):
+            w_t = psum.tile([P, 4, 2 * P], BF16, name="w_t", tag="zT%d" % half)
+            for t in range(4):
+                for c2 in range(2):
+                    nc.tensor.transpose(
+                        w_t[:, t, P * c2 : P * (c2 + 1)],
+                        w2raw[:, 2 * half + c2, P * t : P * (t + 1)],
+                        ident_b[:],
+                    )
+            st[("w_t", half)] = w_t
+
+        def w2_copy(engine, half):
+            engine(
+                out=w2grp[:, 2 * P * half : 2 * P * (half + 1), :],
+                in_=st[("w_t", half)][:].rearrange("p t n -> p n t"),
+            )
+
+        def w2_quantise():
             nc.vector.quantize_mx(
                 out=w2codes[:].bitcast(FP8X4), scales=w2sc[:], in_=w2grp[:].rearrange("p n t -> p (n t)")
             )
+            nc.vector.tensor_copy(out=gam_t[:], in_=gam_raw[:])
+            nc.vector.tensor_copy(out=bet_t[:], in_=bet_raw[:])
 
-        out0_v = out_0.rearrange("(q p j) k -> q p j k", p=P, j=4)
-        out1_v = out_1.rearrange("(q p j) k -> q p j k", p=P, j=4)
-        st = {}
-
-        def stage_a(g):
-            q, j0 = g // 2, 2 * (g % 2)
-            errw = err[q][:].bitcast(F32)
-            xt = psum.tile([P, D], F32, name="xt", tag="xt", bufs=1)
-            for j2 in range(2):
+        def t1(g):
+            errw = err[g][:].bitcast(F32)
+            xt = psum.tile([P, D], F32, name="xt", tag="xt")
+            for j in range(2):
                 for u in range(2):
                     nc.tensor.transpose(
-                        xt[:, 256 * u + P * j2 : 256 * u + P * (j2 + 1)],
-                        errw[:, 256 * (j0 + j2) + P * u : 256 * (j0 + j2) + P * (u + 1)],
+                        xt[:, 256 * u + P * j : 256 * u + P * (j + 1)],
+                        errw[:, 256 * j + P * u : 256 * j + P * (u + 1)],
                         ident_f[:],
                     )
+            st[("xt", g)] = xt
+
+        def a(g):
             g1 = work.tile([P, 2 * D], BF16, name="g1", tag="g1", align_bytes=64)
             nc.vector.tensor_tensor(
                 out=g1[:].rearrange("p (r u e) -> p r u e", u=2, e=2),
-                in0=xt[:].bitcast(BF16).rearrange("p (u r e) -> p r u e", u=2, e=2),
+                in0=st[("xt", g)][:].bitcast(BF16).rearrange("p (u r e) -> p r u e", u=2, e=2),
                 in1=p2w[:].rearrange("p (u e) -> p u e", u=2).unsqueeze(1).to_broadcast([P, 2 * P, 2, 2]),
                 op=ALU.mult,
             )
             st[("g1", g)] = g1
 
-        def stage_b(g):
-            c1 = work.tile([P, 2 * P], U32, name="c1", tag="c1", align_bytes=64)
-            s1 = work.tile([P, 2 * P], U8, name="s1", tag="s1", align_bytes=64)
-            nc.vector.quantize_mx(out=c1[:].bitcast(FP8X4), scales=s1[:], in_=st[("g1", g)][:])
-            for j2 in range(2):
-                cols = slice(P * j2, P * (j2 + 1))
-                g_ps = psum.tile([P, D], F32, name="g_ps", tag="G")
+        def quantise(g, src, tag):
+            codes = work.tile([P, 2 * P], U32, name="codes" + tag, tag="codes" + tag, align_bytes=64)
+            scales = work.tile([P, 2 * P], U8, name="scales" + tag, tag="scales" + tag, align_bytes=64)
+            nc.vector.quantize_mx(out=codes[:].bitcast(FP8X4), scales=scales[:], in_=st[(src, g)][:])
+            st[("q" + tag, g)] = (codes, scales)
+
+        def mx(g, tag, wcodes, wscales):
+            codes, scales = st[("q" + tag, g)]
+            for j in range(2):
+                cols = slice(P * j, P * (j + 1))
+                acc = psum.tile([P, D], F32, name="acc" + tag, tag="acc" + tag, bufs=2)
                 nc.tensor.matmul_mx(
-                    out=g_ps[:],
-                    lhsT=c1[:, cols].bitcast(FP8X4),
-                    lhsT_scale=s1[:, cols],
-                    rhs=w1codes[:].bitcast(FP8X4),
-                    rhs_scale=w1sc[:],
+                    out=acc[:],
+                    lhsT=codes[:, cols].bitcast(FP8X4),
+                    lhsT_scale=scales[:, cols],
+                    rhs=wcodes[:].bitcast(FP8X4),
+                    rhs_scale=wscales[:],
                     start=True,
                     stop=True,
                 )
-                st[("G", g, j2)] = g_ps
+                st[("acc" + tag, g, j)] = acc
 
-        def stage_c(g):
-            q, j0 = g // 2, 2 * (g % 2)
-            sums = small.tile([P, 2], F32, name="sums", tag="sums")
-            for j2 in range(2):
-                u_t = work.tile([P, D], F32, name="u_t", tag="u", bufs=6)
-                nc.vector.scalar_tensor_tensor(
-                    out=u_t[:],
-                    in0=st[("G", g, j2)][:],
-                    scalar=0.2,
-                    in1=hid[q][:, D * (j0 + j2) : D * (j0 + j2 + 1)],
-                    op0=ALU.mult,
-                    op1=ALU.add,
-                    accum_out=sums[:, j2 : j2 + 1],
-                )
-                st[("u", g, j2)] = u_t
-            st[("sums", g)] = sums
+        def c(g, j):
+            if j == 0:
+                st[("sums", g)] = small.tile([P, 2], F32, name="sums", tag="sums")
+            u_t = work.tile([P, D], F32, name="u_t", tag="u", bufs=6)
+            nc.vector.scalar_tensor_tensor(
+                out=u_t[:],
+                in0=st[("acc1", g, j)][:],
+                scalar=0.2,
+                in1=hid[g][:, D * j : D * (j + 1)],
+                op0=ALU.mult,
+                op1=ALU.add,
+                accum_out=st[("sums", g)][:, j : j + 1],
+            )
+            st[("u", g, j)] = u_t
 
-        def stage_d(g):
+        def nm(g):
             negmean = small.tile([P, 2], F32, name="negmean", tag="negmean")
             nc.scalar.mul(out=negmean[:], in_=st[("sums", g)][:], mul=-1.0 / D)
-            ssq = small.tile([P, 2], F32, name="ssq", tag="ssq")
-            for j2 in range(2):
-                junk = work.tile([P, D], BF16, name="junk", tag="junk", bufs=2)
-                nc.scalar.activation(
-                    out=junk[:],
-                    in_=st[("u", g, j2)][:],
-                    func=ACT.Square,
-                    bias=negmean[:, j2 : j2 + 1],
-                    scale=1.0,
-                    accum_out=ssq[:, j2 : j2 + 1],
-                )
+            st[("negmean", g)] = negmean
+            st[("ssq", g)] = small.tile([P, 2], F32, name="ssq", tag="ssq")
+
+        def d(g, j):
+            junk = work.tile([P, D], BF16, name="junk", tag="junk")
+            nc.scalar.activation(
+                out=junk[:],
+                in_=st[("u", g, j)][:],
+                func=ACT.Square,
+                bias=st[("negmean", g)][:, j : j + 1],
+                scale=1.0,
+                accum_out=st[("ssq", g)][:, j : j + 1],
+            )
+
+        def rs(g):
             rstd = small.tile([P, 2], F32, name="rstd", tag="rstd")
             nc.scalar.activation(
-                out=rstd[:], in_=ssq[:], func=ACT.Abs_reciprocal_sqrt, bias=eps_t[:], scale=1.0 / D
+                out=rstd[:], in_=st[("ssq", g)][:], func=ACT.Abs_reciprocal_sqrt, bias=eps_t[:], scale=1.0 / D
             )
-            st[("stats", g)] = (negmean, rstd)
+            st[("rstd", g)] = rstd
 
-        def stage_z(g):
-            negmean, rstd = st[("stats", g)]
-            for j2 in range(2):
-                z_t = work.tile([P, D], F32, name="z_t", tag="z", bufs=4)
-                nc.gpsimd.tensor_scalar(
-                    out=z_t[:],
-                    in0=st[("u", g, j2)][:],
-                    scalar1=negmean[:, j2 : j2 + 1],
-                    scalar2=rstd[:, j2 : j2 + 1],
-                    op0=ALU.add,
-                    op1=ALU.mult,
-                )
-                st[("z", g, j2)] = z_t
+        def z(g, j):
+            z_t = work.tile([P, D], F32, name="z_t", tag="z", bufs=4)
+            nc.gpsimd.tensor_scalar(
+                out=z_t[:],
+                in0=st[("u", g, j)][:],
+                scalar1=st[("negmean", g)][:, j : j + 1],
+                scalar2=st[("rstd", g)][:, j : j + 1],
+                op0=ALU.add,
+                op1=ALU.mult,
+            )
+            st[("z", g, j)] = z_t
 
-        def stage_t(g):
-            hn_t = work.tile([P, 4, 2 * P], F32, name="hn_t", tag="hn_t")
-            for half in range(2):
-                z_ps = psum.tile([P, 2, 2 * P], F32, name="z_ps", tag="zT")
-                for t2 in range(2):
-                    t = 2 * half + t2
-                    for j2 in range(2):
-                        nc.tensor.transpose(
-                            z_ps[:, t2, P * j2 : P * (j2 + 1)], st[("z", g, j2)][:, P * t : P * (t + 1)], ident_f[:]
-                        )
-                for t2 in range(2):
-                    t = 2 * half + t2
-                    nc.scalar.activation(
-                        out=hn_t[:, t, :],
-                        in_=z_ps[:, t2, :],
-                        func=ACT.Identity,
-                        bias=bet_t[:, t : t + 1],
-                        scale=gam_t[:, t : t + 1],
+        def t2(g, half):
+            z_ps = psum.tile([P, 2, 2 * P], F32, name="z_ps", tag="zT%d" % half)
+            for t2i in range(2):
+                t = 2 * half + t2i
+                for j in range(2):
+                    nc.tensor.transpose(
+                        z_ps[:, t2i, P * j : P * (j + 1)], st[("z", g, j)][:, P * t : P * (t + 1)], ident_f[:]
                     )
-            st[("hn_t", g)] = hn_t
+            st[("z_ps", g, half)] = z_ps
 
-        def stage_r(g):
+        def f1(g, half):
+            if half == 0:
+                st[("hn_t", g)] = work.tile([P, 4, 2 * P], F32, name="hn_t", tag="hn_t", bufs=3)
+            for t2i in range(2):
+                t = 2 * half + t2i
+                nc.scalar.activation(
+                    out=st[("hn_t", g)][:, t, :],
+                    in_=st[("z_ps", g, half)][:, t2i, :],
+                    func=ACT.Identity,
+                    bias=bet_t[:, t : t + 1],
+                    scale=gam_t[:, t : t + 1],
+                )
+
+        def r(g):
             g2 = work.tile([P, 2 * D], BF16, name="g2", tag="g2", align_bytes=64)
             nc.gpsimd.tensor_scalar(
                 out=g2[:].rearrange("p (r t) -> p r t", t=4),
@@ -245,56 +259,69 @@ def tile_predictivecodinglayer_pb_t_kernel(
             )
             st[("g2", g)] = g2
 
-        def stage_o(g):
-            q, j0 = g // 2, 2 * (g % 2)
-            hn_t = st[("hn_t", g)]
-            hn = work.tile([P, 2, D], F32, name="hn", tag="hn")
-            for j2 in range(2):
-                h_ps = psum.tile([P, D], F32, name="h_ps", tag="hB", bufs=1)
-                for t in range(4):
-                    nc.tensor.transpose(h_ps[:, P * t : P * (t + 1)], hn_t[:, t, P * j2 : P * (j2 + 1)], ident_f[:])
-                nc.scalar.copy(out=hn[:, j2, :], in_=h_ps[:])
-            nc.sync.dma_start(out=out0_v[q, :, j0 : j0 + 2, :], in_=hn[:])
-
-        def stage_q2(g):
-            c2 = work.tile([P, 2 * P], U32, name="c2", tag="c2", align_bytes=64)
-            s2 = work.tile([P, 2 * P], U8, name="s2", tag="s2", align_bytes=64)
-            nc.vector.quantize_mx(out=c2[:].bitcast(FP8X4), scales=s2[:], in_=st[("g2", g)][:])
-            for j2 in range(2):
-                cols = slice(P * j2, P * (j2 + 1))
-                p_ps = psum.tile([P, D], F32, name="p_ps", tag="P")
-                nc.tensor.matmul_mx(
-                    out=p_ps[:],
-                    lhsT=c2[:, cols].bitcast(FP8X4),
-                    lhsT_scale=s2[:, cols],
-                    rhs=w2codes[:].bitcast(FP8X4),
-                    rhs_scale=w2sc[:],
-                    start=True,
-                    stop=True,
+        def t3(g, j):
+            h_ps = psum.tile([P, D], F32, name="h_ps", tag="hB")
+            for t in range(4):
+                nc.tensor.transpose(
+                    h_ps[:, P * t : P * (t + 1)], st[("hn_t", g)][:, t, P * j : P * (j + 1)], ident_f[:]
                 )
-                st[("P", g, j2)] = p_ps
+            st[("h_ps", g, j)] = h_ps
 
-        def stage_h(g):
-            q, j0 = g // 2, 2 * (g % 2)
-            pred = work.tile([P, 2, D], F32, name="pred", tag="pred")
-            for j2 in range(2):
-                nc.vector.tensor_tensor(out=pred[:, j2, :], in0=st[("P", g, j2)][:], in1=bg_b[:], op=ALU.add)
-            nc.sync.dma_start(out=out1_v[q, :, j0 : j0 + 2, :], in_=pred[:])
+        def o(g, j):
+            if j == 0:
+                st[("hn", g)] = work.tile([P, 2, D], F32, name="hn", tag="hn", bufs=3)
+            nc.scalar.copy(out=st[("hn", g)][:, j, :], in_=st[("h_ps", g, j)][:])
+            if j == 1:
+                nc.sync.dma_start(out=out0_v[g], in_=st[("hn", g)][:])
 
-        def run(stage, g):
+        def h(g, j):
+            if j == 0:
+                st[("pred", g)] = work.tile([P, 2, D], F32, name="pred", tag="pred", bufs=3)
+            nc.vector.tensor_tensor(
+                out=st[("pred", g)][:, j, :], in0=st[("acc2", g, j)][:], in1=bg_b[:], op=ALU.add
+            )
+            if j == 1:
+                nc.sync.dma_start(out=out1_v[g], in_=st[("pred", g)][:])
+
+        def run(stage, g, *args):
             if 0 <= g < PAIRS:
-                stage(g)
+                stage(g, *args)
 
-        for i in range(PAIRS + 4):
-            run(stage_a, i)
-            run(stage_c, i - 1)
-            run(stage_b, i)
-            if i == 0:
-                prepare_w2()
-            run(stage_h, i - 4)
-            run(stage_q2, i - 3)
-            run(stage_d, i - 1)
-            run(stage_t, i - 2)
-            run(stage_o, i - 3)
-            run(stage_z, i - 1)
-            run(stage_r, i - 2)
+        for f in range(-2, PAIRS + 4):
+            run(quantise, f, "g1", "1")
+            run(r, f - 3)
+            run(nm, f - 1)
+            run(d, f - 1, 0)
+            run(mx, f, "1", w1codes, w1sc)
+            if f == 0:
+                w2_transposes(0)
+                w2_transposes(1)
+                w2_copy(nc.scalar.copy, 0)
+            if f == 1:
+                w2_copy(nc.vector.tensor_copy, 1)
+            run(h, f - 4, 0)
+            run(h, f - 4, 1)
+            run(o, f - 3, 0)
+            run(t2, f - 2, 1)
+            run(t3, f - 3, 1)
+            run(c, f, 0)
+            run(d, f - 1, 1)
+            run(rs, f - 1)
+            if f == 1:
+                w2_quantise()
+            run(quantise, f - 3, "g2", "2")
+            run(f1, f - 2, 0)
+            run(z, f - 1, 0)
+            run(z, f - 1, 1)
+            run(mx, f - 3, "2", w2codes, w2sc)
+            run(a, f + 1)
+            if f == -1:
+                nc.vector.quantize_mx(
+                    out=w1codes[:].bitcast(FP8X4), scales=w1sc[:], in_=w1grp[:].rearrange("p n t -> p (n t)")
+                )
+            run(o, f - 3, 1)
+            run(f1, f - 2, 1)
+            run(c, f, 1)
+            run(t1, f + 2)
+            run(t2, f - 1, 0)
+            run(t3, f - 2, 0)

@@ -27,7 +27,7 @@ def tile_predictivecodinglayer_pb_t_kernel(
         consts = ctx.enter_context(tc.tile_pool(name="consts", bufs=1))
         inputs = ctx.enter_context(tc.tile_pool(name="inputs", bufs=1))
         work = ctx.enter_context(tc.tile_pool(name="work", bufs=2))
-        small = ctx.enter_context(tc.tile_pool(name="small", bufs=4))
+        small = ctx.enter_context(tc.tile_pool(name="small", bufs=8))
         psum = ctx.enter_context(tc.psum_pool(name="psum", bufs=1))
         if PINNED:
             ctx.enter_context(tc.manual_schedule())
@@ -176,7 +176,7 @@ def tile_predictivecodinglayer_pb_t_kernel(
         def c(g, j):
             if j == 0:
                 st[("sums", g)] = small.tile([P, 2], F32, name="sums", tag="sums")
-            u_t = work.tile([P, D], F32, name="u_t", tag="u", bufs=6)
+            u_t = work.tile([P, D], F32, name="u_t", tag="u", bufs=10)
             nc.vector.scalar_tensor_tensor(
                 out=u_t[:],
                 in0=st[("acc1", g, j)][:],
@@ -213,7 +213,7 @@ def tile_predictivecodinglayer_pb_t_kernel(
             st[("rstd", g)] = rstd
 
         def z(g, j):
-            z_t = work.tile([P, D], F32, name="z_t", tag="z", bufs=4)
+            z_t = work.tile([P, D], F32, name="z_t", tag="z", bufs=6)
             nc.gpsimd.tensor_scalar(
                 out=z_t[:],
                 in0=st[("u", g, j)][:],
@@ -236,7 +236,7 @@ def tile_predictivecodinglayer_pb_t_kernel(
 
         def f1(g, half):
             if half == 0:
-                st[("hn_t", g)] = work.tile([P, 4, 2 * P], F32, name="hn_t", tag="hn_t", bufs=3)
+                st[("hn_t", g)] = work.tile([P, 4, 2 * P], F32, name="hn_t", tag="hn_t", bufs=4)
             for t2i in range(2):
                 t = 2 * half + t2i
                 nc.scalar.activation(
@@ -248,7 +248,7 @@ def tile_predictivecodinglayer_pb_t_kernel(
                 )
 
         def r(g):
-            g2 = work.tile([P, 2 * D], BF16, name="g2", tag="g2", align_bytes=64)
+            g2 = work.tile([P, 2 * D], BF16, name="g2", tag="g2", align_bytes=64, bufs=4)
             nc.gpsimd.tensor_scalar(
                 out=g2[:].rearrange("p (r t) -> p r t", t=4),
                 in0=st[("hn_t", g)][:].rearrange("p t r -> p r t"),
@@ -288,40 +288,40 @@ def tile_predictivecodinglayer_pb_t_kernel(
                 stage(g, *args)
 
         for f in range(-2, PAIRS + 4):
-            run(quantise, f, "g1", "1")
-            run(r, f - 3)
             run(nm, f - 1)
-            run(d, f - 1, 0)
-            run(mx, f, "1", w1codes, w1sc)
-            if f == 0:
-                w2_transposes(0)
-                w2_transposes(1)
-                w2_copy(nc.scalar.copy, 0)
-            if f == 1:
-                w2_copy(nc.vector.tensor_copy, 1)
-            run(h, f - 4, 0)
-            run(h, f - 4, 1)
-            run(o, f - 3, 0)
-            run(t2, f - 2, 1)
-            run(t3, f - 3, 1)
-            run(c, f, 0)
+            run(quantise, f, "g1", "1")
             run(d, f - 1, 1)
-            run(rs, f - 1)
-            if f == 1:
-                w2_quantise()
-            run(quantise, f - 3, "g2", "2")
-            run(f1, f - 2, 0)
-            run(z, f - 1, 0)
-            run(z, f - 1, 1)
-            run(mx, f - 3, "2", w2codes, w2sc)
             run(a, f + 1)
             if f == -1:
                 nc.vector.quantize_mx(
                     out=w1codes[:].bitcast(FP8X4), scales=w1sc[:], in_=w1grp[:].rearrange("p n t -> p (n t)")
                 )
-            run(o, f - 3, 1)
+            run(t2, f - 2, 1)
+            run(d, f - 1, 0)
+            if f == 1:
+                w2_copy(nc.vector.tensor_copy, 1)
+            run(h, f - 4, 0)
+            run(mx, f, "1", w1codes, w1sc)
+            if f == 0:
+                w2_transposes(0)
+                w2_transposes(1)
+                w2_copy(nc.scalar.copy, 0)
+            run(rs, f - 1)
+            run(r, f - 3)
+            run(t1, f + 2)
+            run(h, f - 4, 1)
+            if f == 1:
+                w2_quantise()
+            run(quantise, f - 3, "g2", "2")
+            run(z, f - 1, 1)
+            run(o, f - 3, 0)
+            run(t3, f - 3, 1)
+            run(f1, f - 2, 0)
+            run(mx, f - 3, "2", w2codes, w2sc)
+            run(z, f - 1, 0)
+            run(c, f, 0)
             run(f1, f - 2, 1)
             run(c, f, 1)
-            run(t1, f + 2)
+            run(o, f - 3, 1)
             run(t2, f - 1, 0)
             run(t3, f - 2, 0)

@@ -87,7 +87,7 @@ def tile_predictivecodinglayer_pb_t_kernel(
         lnv = consts.tile([P, 4], F32, name="lnv")
         nc.scalar.activation(out=lnv[:], in_=expv[:], func=ACT.Ln, bias=one_t[:], scale=1.0)
         warm = consts.tile([P, 1], F32, name="warm")
-        nc.scalar.activation(out=warm[:], in_=one_t[:], func=ACT.Abs_reciprocal_sqrt)
+        nc.scalar.activation(out=warm[:], in_=one_t[:], func=ACT.Sqrt)
         spv = consts.tile([P, 4], F32, name="spv")
         nc.vector.scalar_tensor_tensor(
             out=spv[:], in0=lp[:], scalar=0.0, in1=lnv[:], op0=ALU.max, op1=ALU.add
@@ -206,10 +206,13 @@ def tile_predictivecodinglayer_pb_t_kernel(
             )
 
         def rs(g):
+            std = small.tile([P, 2], F32, name="std", tag="std")
+            nc.scalar.activation(out=std[:], in_=st[("ssq", g)][:], func=ACT.Sqrt, bias=eps_t[:], scale=1.0 / D)
+            st[("std", g)] = std
+
+        def rc(g):
             rstd = small.tile([P, 2], F32, name="rstd", tag="rstd")
-            nc.scalar.activation(
-                out=rstd[:], in_=st[("ssq", g)][:], func=ACT.Abs_reciprocal_sqrt, bias=eps_t[:], scale=1.0 / D
-            )
+            nc.vector.reciprocal(out=rstd[:], in_=st[("std", g)][:])
             st[("rstd", g)] = rstd
 
         def z(g, j):
@@ -310,6 +313,7 @@ def tile_predictivecodinglayer_pb_t_kernel(
             run(r, f - 3)
             run(t1, f + 2)
             run(h, f - 4, 1)
+            run(rc, f - 1)
             if f == 1:
                 w2_quantise()
             run(quantise, f - 3, "g2", "2")

@@ -16,7 +16,6 @@ B = 4096
 D = 512
 PAIRS = B // (2 * P)
 FLOPS = 2 * 2 * B * D * D
-PINNED = True
 
 
 def tile_predictivecodinglayer_pb_t_kernel(
@@ -29,8 +28,7 @@ def tile_predictivecodinglayer_pb_t_kernel(
         work = ctx.enter_context(tc.tile_pool(name="work", bufs=2))
         small = ctx.enter_context(tc.tile_pool(name="small", bufs=8))
         psum = ctx.enter_context(tc.psum_pool(name="psum", bufs=1))
-        if PINNED:
-            ctx.enter_context(tc.manual_schedule())
+        ctx.enter_context(tc.manual_schedule())
 
         err_v = error.rearrange("(g p j) k -> g p (j k)", p=P, j=2)
         hid_v = hidden.rearrange("(g p j) k -> g p (j k)", p=P, j=2)
@@ -192,22 +190,23 @@ def tile_predictivecodinglayer_pb_t_kernel(
             negmean = small.tile([P, 2], F32, name="negmean", tag="negmean")
             nc.scalar.mul(out=negmean[:], in_=st[("sums", g)][:], mul=-1.0 / D)
             st[("negmean", g)] = negmean
-            st[("ssq", g)] = small.tile([P, 2], F32, name="ssq", tag="ssq")
 
         def d(g, j):
+            if j == 0:
+                st[("ssq", g)] = small.tile([P, 2], F32, name="ssq", tag="ssq")
             junk = work.tile([P, D], BF16, name="junk", tag="junk")
             nc.scalar.activation(
                 out=junk[:],
                 in_=st[("u", g, j)][:],
                 func=ACT.Square,
-                bias=st[("negmean", g)][:, j : j + 1],
-                scale=1.0,
+                bias=st[("sums", g)][:, j : j + 1],
+                scale=-float(D),
                 accum_out=st[("ssq", g)][:, j : j + 1],
             )
 
         def rs(g):
             std = small.tile([P, 2], F32, name="std", tag="std")
-            nc.scalar.activation(out=std[:], in_=st[("ssq", g)][:], func=ACT.Sqrt, bias=eps_t[:], scale=1.0 / D)
+            nc.scalar.activation(out=std[:], in_=st[("ssq", g)][:], func=ACT.Sqrt, bias=eps_t[:], scale=1.0 / D**3)
             st[("std", g)] = std
 
         def rc(g):
@@ -215,9 +214,9 @@ def tile_predictivecodinglayer_pb_t_kernel(
             nc.vector.reciprocal(out=rstd[:], in_=st[("std", g)][:])
             st[("rstd", g)] = rstd
 
-        def z(g, j):
-            z_t = work.tile([P, D], F32, name="z_t", tag="z", bufs=6)
-            nc.gpsimd.tensor_scalar(
+        def z(g, j, engine=nc.gpsimd):
+            z_t = work.tile([P, D], F32, name="z_t", tag="z", bufs=8)
+            engine.tensor_scalar(
                 out=z_t[:],
                 in0=st[("u", g, j)][:],
                 scalar1=st[("negmean", g)][:, j : j + 1],
@@ -227,8 +226,9 @@ def tile_predictivecodinglayer_pb_t_kernel(
             )
             st[("z", g, j)] = z_t
 
-        def t2(g, half):
-            z_ps = psum.tile([P, 2, 2 * P], F32, name="z_ps", tag="zT%d" % half)
+        def t2(g, half, bank=None):
+            bank = bank or "zT%d" % half
+            z_ps = psum.tile([P, 2, 2 * P], F32, name="z_ps", tag=bank, bufs=2 if bank == "acc1" else 1)
             for t2i in range(2):
                 t = 2 * half + t2i
                 for j in range(2):
@@ -250,9 +250,9 @@ def tile_predictivecodinglayer_pb_t_kernel(
                     scale=gam_t[:, t : t + 1],
                 )
 
-        def r(g):
+        def r(g, engine=nc.gpsimd):
             g2 = work.tile([P, 2 * D], BF16, name="g2", tag="g2", align_bytes=64, bufs=4)
-            nc.gpsimd.tensor_scalar(
+            engine.tensor_scalar(
                 out=g2[:].rearrange("p (r t) -> p r t", t=4),
                 in0=st[("hn_t", g)][:].rearrange("p t r -> p r t"),
                 scalar1=1.0,
@@ -262,8 +262,8 @@ def tile_predictivecodinglayer_pb_t_kernel(
             )
             st[("g2", g)] = g2
 
-        def t3(g, j):
-            h_ps = psum.tile([P, D], F32, name="h_ps", tag="hB")
+        def t3(g, j, bank="hB"):
+            h_ps = psum.tile([P, D], F32, name="h_ps", tag=bank, bufs=2 if bank == "acc1" else 1)
             for t in range(4):
                 nc.tensor.transpose(
                     h_ps[:, P * t : P * (t + 1)], st[("hn_t", g)][:, t, P * j : P * (j + 1)], ident_f[:]
@@ -272,44 +272,50 @@ def tile_predictivecodinglayer_pb_t_kernel(
 
         def o(g, j):
             if j == 0:
-                st[("hn", g)] = work.tile([P, 2, D], F32, name="hn", tag="hn", bufs=3)
+                st[("hn", g)] = work.tile([P, 2, D], F32, name="hn", tag="hn", bufs=4)
             nc.scalar.copy(out=st[("hn", g)][:, j, :], in_=st[("h_ps", g, j)][:])
-            if j == 1:
+            if g >= PAIRS - 2:
+                nc.sync.dma_start(out=out0_v[g][:, j], in_=st[("hn", g)][:, j])
+            elif j == 1:
                 nc.sync.dma_start(out=out0_v[g], in_=st[("hn", g)][:])
 
         def h(g, j):
             if j == 0:
-                st[("pred", g)] = work.tile([P, 2, D], F32, name="pred", tag="pred", bufs=3)
+                st[("pred", g)] = work.tile([P, 2, D], F32, name="pred", tag="pred", bufs=4)
             nc.vector.tensor_tensor(
                 out=st[("pred", g)][:, j, :], in0=st[("acc2", g, j)][:], in1=bg_b[:], op=ALU.add
             )
-            if j == 1:
+            if g >= PAIRS - 2:
+                nc.sync.dma_start(out=out1_v[g][:, j], in_=st[("pred", g)][:, j])
+            elif j == 1:
                 nc.sync.dma_start(out=out1_v[g], in_=st[("pred", g)][:])
 
         def run(stage, g, *args):
             if 0 <= g < PAIRS:
                 stage(g, *args)
 
-        for f in range(-2, PAIRS + 4):
-            run(nm, f - 1)
-            run(quantise, f, "g1", "1")
-            run(d, f - 1, 1)
+        for f in range(-2, PAIRS):
+            run(d, f - 1, 0)
             run(a, f + 1)
             if f == -1:
                 nc.vector.quantize_mx(
                     out=w1codes[:].bitcast(FP8X4), scales=w1sc[:], in_=w1grp[:].rearrange("p n t -> p (n t)")
                 )
             run(t2, f - 2, 1)
-            run(d, f - 1, 0)
-            if f == 1:
-                w2_copy(nc.vector.tensor_copy, 1)
+            run(d, f - 1, 1)
             run(h, f - 4, 0)
             run(mx, f, "1", w1codes, w1sc)
+            if f < 2:
+                run(c, f, 0)
+                run(c, f, 1)
             if f == 0:
                 w2_transposes(0)
                 w2_transposes(1)
-                w2_copy(nc.scalar.copy, 0)
             run(rs, f - 1)
+            run(nm, f - 1)
+            if f == 1:
+                w2_copy(nc.scalar.copy, 0)
+                w2_copy(nc.scalar.copy, 1)
             run(r, f - 3)
             run(t1, f + 2)
             run(h, f - 4, 1)
@@ -317,15 +323,60 @@ def tile_predictivecodinglayer_pb_t_kernel(
             if f == 1:
                 w2_quantise()
             run(quantise, f - 3, "g2", "2")
+            run(quantise, f + 1, "g1", "1")
             run(z, f - 1, 1)
             run(o, f - 3, 0)
             run(t3, f - 3, 1)
             run(f1, f - 2, 0)
             run(mx, f - 3, "2", w2codes, w2sc)
             run(z, f - 1, 0)
-            run(c, f, 0)
+            if f >= 2:
+                run(c, f, 0)
+                run(c, f, 1)
             run(f1, f - 2, 1)
-            run(c, f, 1)
             run(o, f - 3, 1)
             run(t2, f - 1, 0)
             run(t3, f - 2, 0)
+        y, x, w, v = PAIRS - 1, PAIRS - 2, PAIRS - 3, PAIRS - 4
+        d(y, 0)
+        d(y, 1)
+        t2(x, 1)
+        o(w, 0)
+        rs(y)
+        nm(y)
+        r(w)
+        h(v, 0)
+        h(v, 1)
+        quantise(w, "g2", "2")
+        mx(w, "2", w2codes, w2sc)
+        t3(w, 1, "acc1")
+        f1(x, 0)
+        f1(x, 1)
+        rc(y)
+        z(y, 0, nc.vector)
+        z(y, 1, nc.vector)
+        t2(y, 0, "xt")
+        t2(y, 1, "acc1")
+        r(x)
+        o(w, 1)
+        h(w, 0)
+        h(w, 1)
+        f1(y, 0)
+        f1(y, 1)
+        t3(x, 0)
+        t3(x, 1, "acc1")
+        quantise(x, "g2", "2")
+        mx(x, "2", w2codes, w2sc)
+        r(y, nc.vector)
+        o(x, 0)
+        h(x, 0)
+        quantise(y, "g2", "2")
+        o(x, 1)
+        h(x, 1)
+        t3(y, 0, "zT0")
+        t3(y, 1, "zT1")
+        mx(y, "2", w2codes, w2sc)
+        o(y, 0)
+        o(y, 1)
+        h(y, 0)
+        h(y, 1)

@@ -76,7 +76,8 @@ def tile_predictivecodinglayer_pb_t_kernel(
         nc.vector.memset(one_t[:], 1.0)
 
         w1grp = consts.tile([P, D, 4], BF16, name="w1grp", align_bytes=64)
-        nc.vector.tensor_copy(out=w1grp[:], in_=w1raw[:].rearrange("p t n -> p n t"))
+        half = D // 2
+        nc.vector.tensor_copy(out=w1grp[:, 0:half, :], in_=w1raw[:, :, 0:half].rearrange("p t n -> p n t"))
 
         absv = consts.tile([P, 4], F32, name="absv")
         nc.scalar.activation(out=absv[:], in_=lp[:], func=ACT.Abs)
@@ -84,6 +85,7 @@ def tile_predictivecodinglayer_pb_t_kernel(
         nc.scalar.activation(out=expv[:], in_=absv[:], func=ACT.Exp, scale=-1.0)
         lnv = consts.tile([P, 4], F32, name="lnv")
         nc.scalar.activation(out=lnv[:], in_=expv[:], func=ACT.Ln, bias=one_t[:], scale=1.0)
+        nc.scalar.copy(out=w1grp[:, half:D, :], in_=w1raw[:, :, half:D].rearrange("p t n -> p n t"))
         warm = consts.tile([P, 1], F32, name="warm")
         nc.scalar.activation(out=warm[:], in_=one_t[:], func=ACT.Sqrt)
         spv = consts.tile([P, 4], F32, name="spv")
@@ -320,10 +322,10 @@ def tile_predictivecodinglayer_pb_t_kernel(
             run(t1, f + 2)
             run(h, f - 4, 1)
             run(rc, f - 1)
-            if f == 1:
-                w2_quantise()
             run(quantise, f - 3, "g2", "2")
             run(quantise, f + 1, "g1", "1")
+            if f == 1:
+                w2_quantise()
             run(z, f - 1, 1)
             run(o, f - 3, 0)
             run(t3, f - 3, 1)
@@ -341,6 +343,7 @@ def tile_predictivecodinglayer_pb_t_kernel(
         d(y, 0)
         d(y, 1)
         t2(x, 1)
+        t3(w, 1, "acc1")
         o(w, 0)
         rs(y)
         nm(y)
@@ -349,7 +352,6 @@ def tile_predictivecodinglayer_pb_t_kernel(
         h(v, 1)
         quantise(w, "g2", "2")
         mx(w, "2", w2codes, w2sc)
-        t3(w, 1, "acc1")
         f1(x, 0)
         f1(x, 1)
         rc(y)
@@ -357,7 +359,6 @@ def tile_predictivecodinglayer_pb_t_kernel(
         z(y, 1, nc.vector)
         t2(y, 0, "xt")
         t2(y, 1, "acc1")
-        r(x)
         o(w, 1)
         h(w, 0)
         h(w, 1)
@@ -365,6 +366,7 @@ def tile_predictivecodinglayer_pb_t_kernel(
         f1(y, 1)
         t3(x, 0)
         t3(x, 1, "acc1")
+        r(x, nc.vector)
         quantise(x, "g2", "2")
         mx(x, "2", w2codes, w2sc)
         r(y, nc.vector)

@@ -255,8 +255,8 @@ def tile_predictivecodinglayer_pb_t_kernel(
         def r(g, engine=nc.gpsimd):
             g2 = work.tile([P, 2 * D], BF16, name="g2", tag="g2", align_bytes=64, bufs=4)
             engine.tensor_scalar(
-                out=g2[:].rearrange("p (r t) -> p r t", t=4),
-                in0=st[("hn_t", g)][:].rearrange("p t r -> p r t"),
+                out=g2[:].rearrange("p (c i t) -> p c t i", i=4, t=4),
+                in0=st[("hn_t", g)][:].rearrange("p t (c i) -> p c t i", i=4),
                 scalar1=1.0,
                 scalar2=0.0,
                 op0=ALU.mult,

@@ -79,21 +79,22 @@ def tile_predictivecodinglayer_pb_t_kernel(
         half = D // 2
         nc.vector.tensor_copy(out=w1grp[:, 0:half, :], in_=w1raw[:, :, 0:half].rearrange("p t n -> p n t"))
 
+        posv = consts.tile([P, 4], F32, name="posv")
+        nc.scalar.activation(out=posv[:], in_=lp[:], func=ACT.Relu)
         absv = consts.tile([P, 4], F32, name="absv")
         nc.scalar.activation(out=absv[:], in_=lp[:], func=ACT.Abs)
         expv = consts.tile([P, 4], F32, name="expv")
         nc.scalar.activation(out=expv[:], in_=absv[:], func=ACT.Exp, scale=-1.0)
         lnv = consts.tile([P, 4], F32, name="lnv")
         nc.scalar.activation(out=lnv[:], in_=expv[:], func=ACT.Ln, bias=one_t[:], scale=1.0)
+        p2w = consts.tile([P, 4], F32, name="p2w")
+        for t in range(4):
+            nc.scalar.activation(
+                out=p2w[:, t : t + 1], in_=lnv[:, t : t + 1], func=ACT.Square, bias=posv[:, t : t + 1], scale=1.0
+            )
         nc.scalar.copy(out=w1grp[:, half:D, :], in_=w1raw[:, :, half:D].rearrange("p t n -> p n t"))
         warm = consts.tile([P, 1], F32, name="warm")
         nc.scalar.activation(out=warm[:], in_=one_t[:], func=ACT.Sqrt)
-        spv = consts.tile([P, 4], F32, name="spv")
-        nc.vector.scalar_tensor_tensor(
-            out=spv[:], in0=lp[:], scalar=0.0, in1=lnv[:], op0=ALU.max, op1=ALU.add
-        )
-        p2w = consts.tile([P, 4], F32, name="p2w")
-        nc.vector.tensor_tensor(out=p2w[:], in0=spv[:], in1=spv[:], op=ALU.mult)
 
         w1codes = consts.tile([P, D], U32, name="w1codes", align_bytes=64)
         w1sc = consts.tile([P, D], U8, name="w1sc", align_bytes=64)
@@ -103,6 +104,8 @@ def tile_predictivecodinglayer_pb_t_kernel(
         w2sc = consts.tile([P, D], U8, name="w2sc", align_bytes=64)
         gam_t = consts.tile([P, 4], F32, name="gam_t")
         bet_t = consts.tile([P, 4], F32, name="bet_t")
+        nc.gpsimd.tensor_copy(out=gam_t[:], in_=gam_raw[:])
+        nc.gpsimd.tensor_copy(out=bet_t[:], in_=bet_raw[:])
         st = {}
 
         def w2_transposes(half):
@@ -126,8 +129,6 @@ def tile_predictivecodinglayer_pb_t_kernel(
             nc.vector.quantize_mx(
                 out=w2codes[:].bitcast(FP8X4), scales=w2sc[:], in_=w2grp[:].rearrange("p n t -> p (n t)")
             )
-            nc.vector.tensor_copy(out=gam_t[:], in_=gam_raw[:])
-            nc.vector.tensor_copy(out=bet_t[:], in_=bet_raw[:])
 
         def t1(g):
             errw = err[g][:].bitcast(F32)
@@ -276,7 +277,7 @@ def tile_predictivecodinglayer_pb_t_kernel(
             if j == 0:
                 st[("hn", g)] = work.tile([P, 2, D], F32, name="hn", tag="hn", bufs=4)
             nc.scalar.copy(out=st[("hn", g)][:, j, :], in_=st[("h_ps", g, j)][:])
-            if g >= PAIRS - 2:
+            if g >= PAIRS - 3:
                 nc.sync.dma_start(out=out0_v[g][:, j], in_=st[("hn", g)][:, j])
             elif j == 1:
                 nc.sync.dma_start(out=out0_v[g], in_=st[("hn", g)][:])
@@ -287,7 +288,7 @@ def tile_predictivecodinglayer_pb_t_kernel(
             nc.vector.tensor_tensor(
                 out=st[("pred", g)][:, j, :], in0=st[("acc2", g, j)][:], in1=bg_b[:], op=ALU.add
             )
-            if g >= PAIRS - 2:
+            if g >= PAIRS - 3:
                 nc.sync.dma_start(out=out1_v[g][:, j], in_=st[("pred", g)][:, j])
             elif j == 1:
                 nc.sync.dma_start(out=out1_v[g], in_=st[("pred", g)][:])
@@ -296,35 +297,39 @@ def tile_predictivecodinglayer_pb_t_kernel(
             if 0 <= g < PAIRS:
                 stage(g, *args)
 
-        for f in range(-2, PAIRS):
+        t1(0)
+        a(0)
+        t1(1)
+        nc.vector.quantize_mx(
+            out=w1codes[:].bitcast(FP8X4), scales=w1sc[:], in_=w1grp[:].rearrange("p n t -> p (n t)")
+        )
+        quantise(0, "g1", "1")
+        mx(0, "1", w1codes, w1sc)
+        a(1)
+        t1(2)
+        w2_transposes(0)
+        w2_transposes(1)
+        for f in range(PAIRS):
             run(d, f - 1, 0)
-            run(a, f + 1)
-            if f == -1:
-                nc.vector.quantize_mx(
-                    out=w1codes[:].bitcast(FP8X4), scales=w1sc[:], in_=w1grp[:].rearrange("p n t -> p (n t)")
-                )
             run(t2, f - 2, 1)
             run(d, f - 1, 1)
-            run(h, f - 4, 0)
-            run(mx, f, "1", w1codes, w1sc)
-            if f < 2:
-                run(c, f, 0)
-                run(c, f, 1)
-            if f == 0:
-                w2_transposes(0)
-                w2_transposes(1)
+            if 1 <= f and f not in (2, 3):
+                run(mx, f, "1", w1codes, w1sc)
             run(rs, f - 1)
             run(nm, f - 1)
             if f == 1:
                 w2_copy(nc.scalar.copy, 0)
                 w2_copy(nc.scalar.copy, 1)
             run(r, f - 3)
-            run(t1, f + 2)
-            run(h, f - 4, 1)
+            if f >= 1:
+                run(t1, f + 2)
+            if f in (0,):
+                run(c, f, 0)
+                run(c, f, 1)
             run(rc, f - 1)
             run(quantise, f - 3, "g2", "2")
             run(quantise, f + 1, "g1", "1")
-            if f == 1:
+            if f == 2:
                 w2_quantise()
             run(z, f - 1, 1)
             run(o, f - 3, 0)
@@ -332,11 +337,16 @@ def tile_predictivecodinglayer_pb_t_kernel(
             run(f1, f - 2, 0)
             run(mx, f - 3, "2", w2codes, w2sc)
             run(z, f - 1, 0)
-            if f >= 2:
+            if f not in (0,):
                 run(c, f, 0)
                 run(c, f, 1)
+            run(h, f - 3, 0)
+            run(h, f - 3, 1)
+            run(a, f + 2)
             run(f1, f - 2, 1)
             run(o, f - 3, 1)
+            if f + 1 in (2, 3):
+                run(mx, f + 1, "1", w1codes, w1sc)
             run(t2, f - 1, 0)
             run(t3, f - 2, 0)
         y, x, w, v = PAIRS - 1, PAIRS - 2, PAIRS - 3, PAIRS - 4
@@ -348,8 +358,6 @@ def tile_predictivecodinglayer_pb_t_kernel(
         rs(y)
         nm(y)
         r(w)
-        h(v, 0)
-        h(v, 1)
         quantise(w, "g2", "2")
         mx(w, "2", w2codes, w2sc)
         f1(x, 0)
@@ -371,12 +379,12 @@ def tile_predictivecodinglayer_pb_t_kernel(
         mx(x, "2", w2codes, w2sc)
         r(y, nc.vector)
         o(x, 0)
+        o(x, 1)
         h(x, 0)
         quantise(y, "g2", "2")
-        o(x, 1)
-        h(x, 1)
         t3(y, 0, "zT0")
         t3(y, 1, "zT1")
+        h(x, 1)
         mx(y, "2", w2codes, w2sc)
         o(y, 0)
         o(y, 1)

from contextlib import ExitStack

import concourse.mybir as mybir
from concourse.masks import make_identity

F32 = mybir.dt.float32
BF16 = mybir.dt.bfloat16
U32 = mybir.dt.uint32
U8 = mybir.dt.uint8
FP8X4 = mybir.dt.float8_e4m3fn_x4
ALU = mybir.AluOpType
ACT = mybir.ActivationFunctionType

P = 128
B = 4096
D = 512
PAIRS = B // (2 * P)
FLOPS = 2 * 2 * B * D * D


def tile_predictivecodinglayer_pb_t_kernel(
    tc, hidden, error, Wg, bg, log_precision, gamma, beta, out_0, out_1
):
    nc = tc.nc
    with ExitStack() as ctx:
        consts = ctx.enter_context(tc.tile_pool(name="consts", bufs=1))
        inputs = ctx.enter_context(tc.tile_pool(name="inputs", bufs=1))
        work = ctx.enter_context(tc.tile_pool(name="work", bufs=2))
        small = ctx.enter_context(tc.tile_pool(name="small", bufs=8))
        psum = ctx.enter_context(tc.psum_pool(name="psum", bufs=1))
        ctx.enter_context(tc.manual_schedule())

        err_v = error.rearrange("(g p j) k -> g p (j k)", p=P, j=2)
        hid_v = hidden.rearrange("(g p j) k -> g p (j k)", p=P, j=2)
        out0_v = out_0.rearrange("(g p j) k -> g p j k", p=P, j=2)
        out1_v = out_1.rearrange("(g p j) k -> g p j k", p=P, j=2)
        lp = consts.tile([P, 4], BF16, name="lp")
        nc.sync.dma_start(
            out=lp[:].rearrange("p (u e) -> p u e", u=2),
            in_=log_precision.rearrange("(u p e) -> p u e", u=2, e=2),
        )
        w1raw = consts.tile([P, 4, D], BF16, name="w1raw")
        w2raw = consts.tile([P, 4, D], BF16, name="w2raw")
        gam_raw = consts.tile([P, 4], BF16, name="gam_raw")
        bet_raw = consts.tile([P, 4], BF16, name="bet_raw")
        bg_b = consts.tile([P, D], BF16, name="bg_b")
        nc.sync.dma_start(
            out=w1raw[:].rearrange("p (u e) n -> p u e n", u=2),
            in_=Wg.rearrange("(u p e) n -> p u e n", u=2, e=2),
        )
        err = []
        hid = []
        for g in range(PAIRS):
            err_g = inputs.tile([P, 2 * D], BF16, name="err%d" % g)
            nc.sync.dma_start(out=err_g[:], in_=err_v[g])
            err.append(err_g)
            hid_g = inputs.tile([P, 2 * D], BF16, name="hid%d" % g)
            nc.sync.dma_start(out=hid_g[:], in_=hid_v[g])
            hid.append(hid_g)
            if g == 0:
                nc.sync.dma_start(out=w2raw[:], in_=Wg.rearrange("(c p) k -> p c k", p=P))
            if g == 1:
                with nc.allow_non_contiguous_dma(reason="two vectors of 512, one element to a partition, once"):
                    nc.sync.dma_start(out=gam_raw[:], in_=gamma.rearrange("(t p) -> p t", p=P))
                    nc.sync.dma_start(out=bet_raw[:], in_=beta.rearrange("(t p) -> p t", p=P))
            if g == 2:
                nc.sync.dma_start(out=bg_b[:], in_=bg.partition_broadcast(P))

        ident_f = consts.tile([P, P], F32, name="ident_f")
        make_identity(nc, ident_f[:])
        ident_b = consts.tile([P, P], BF16, name="ident_b")
        make_identity(nc, ident_b[:])
        eps_t = consts.tile([P, 1], F32, name="eps_t")
        nc.vector.memset(eps_t[:], 1e-5)
        one_t = consts.tile([P, 1], F32, name="one_t")
        nc.vector.memset(one_t[:], 1.0)

        w1grp = consts.tile([P, D, 4], BF16, name="w1grp", align_bytes=64)
        half = D // 2
        nc.vector.tensor_copy(out=w1grp[:, 0:half, :], in_=w1raw[:, :, 0:half].rearrange("p t n -> p n t"))

        posv = consts.tile([P, 4], F32, name="posv")
        nc.scalar.activation(out=posv[:], in_=lp[:], func=ACT.Relu)
        absv = consts.tile([P, 4], F32, name="absv")
        nc.scalar.activation(out=absv[:], in_=lp[:], func=ACT.Abs)
        expv = consts.tile([P, 4], F32, name="expv")
        nc.scalar.activation(out=expv[:], in_=absv[:], func=ACT.Exp, scale=-1.0)
        lnv = consts.tile([P, 4], F32, name="lnv")
        nc.scalar.activation(out=lnv[:], in_=expv[:], func=ACT.Ln, bias=one_t[:], scale=1.0)
        p2w = consts.tile([P, 4], F32, name="p2w")
        for t in range(4):
            nc.scalar.activation(
                out=p2w[:, t : t + 1], in_=lnv[:, t : t + 1], func=ACT.Square, bias=posv[:, t : t + 1], scale=1.0
            )
        nc.scalar.copy(out=w1grp[:, half:D, :], in_=w1raw[:, :, half:D].rearrange("p t n -> p n t"))
        warm = consts.tile([P, 1], F32, name="warm")
        nc.scalar.activation(out=warm[:], in_=one_t[:], func=ACT.Sqrt)

        w1codes = consts.tile([P, D], U32, name="w1codes", align_bytes=64)
        w1sc = consts.tile([P, D], U8, name="w1sc", align_bytes=64)

        w2grp = consts.tile([P, D, 4], BF16, name="w2grp", align_bytes=64)
        w2codes = consts.tile([P, D], U32, name="w2codes", align_bytes=64)
        w2sc = consts.tile([P, D], U8, name="w2sc", align_bytes=64)
        gam_t = consts.tile([P, 4], F32, name="gam_t")
        bet_t = consts.tile([P, 4], F32, name="bet_t")
        nc.gpsimd.tensor_copy(out=gam_t[:], in_=gam_raw[:])
        nc.gpsimd.tensor_copy(out=bet_t[:], in_=bet_raw[:])
        st = {}

        def w2_transposes(half):
            w_t = psum.tile([P, 4, 2 * P], BF16, name="w_t", tag="zT%d" % half)
            for t in range(4):
                for c2 in range(2):
                    nc.tensor.transpose(
                        w_t[:, t, P * c2 : P * (c2 + 1)],
                        w2raw[:, 2 * half + c2, P * t : P * (t + 1)],
                        ident_b[:],
                    )
            st[("w_t", half)] = w_t

        def w2_copy(engine, half):
            engine(
                out=w2grp[:, 2 * P * half : 2 * P * (half + 1), :],
                in_=st[("w_t", half)][:].rearrange("p t n -> p n t"),
            )

        def w2_quantise():
            nc.vector.quantize_mx(
                out=w2codes[:].bitcast(FP8X4), scales=w2sc[:], in_=w2grp[:].rearrange("p n t -> p (n t)")
            )

        def t1(g):
            errw = err[g][:].bitcast(F32)
            xt = psum.tile([P, D], F32, name="xt", tag="xt")
            for j in range(2):
                for u in range(2):
                    nc.tensor.transpose(
                        xt[:, 256 * u + P * j : 256 * u + P * (j + 1)],
                        errw[:, 256 * j + P * u : 256 * j + P * (u + 1)],
                        ident_f[:],
                    )
            st[("xt", g)] = xt

        def a(g):
            g1 = work.tile([P, 2 * D], BF16, name="g1", tag="g1", align_bytes=64)
            nc.vector.tensor_tensor(
                out=g1[:].rearrange("p (r u e) -> p r u e", u=2, e=2),
                in0=st[("xt", g)][:].bitcast(BF16).rearrange("p (u r e) -> p r u e", u=2, e=2),
                in1=p2w[:].rearrange("p (u e) -> p u e", u=2).unsqueeze(1).to_broadcast([P, 2 * P, 2, 2]),
                op=ALU.mult,
            )
            st[("g1", g)] = g1

        def quantise(g, src, tag):
            codes = work.tile([P, 2 * P], U32, name="codes" + tag, tag="codes" + tag, align_bytes=64)
            scales = work.tile([P, 2 * P], U8, name="scales" + tag, tag="scales" + tag, align_bytes=64)
            nc.vector.quantize_mx(out=codes[:].bitcast(FP8X4), scales=scales[:], in_=st[(src, g)][:])
            st[("q" + tag, g)] = (codes, scales)

        def mx(g, tag, wcodes, wscales):
            codes, scales = st[("q" + tag, g)]
            for j in range(2):
                cols = slice(P * j, P * (j + 1))
                acc = psum.tile([P, D], F32, name="acc" + tag, tag="acc" + tag, bufs=2)
                nc.tensor.matmul_mx(
                    out=acc[:],
                    lhsT=codes[:, cols].bitcast(FP8X4),
                    lhsT_scale=scales[:, cols],
                    rhs=wcodes[:].bitcast(FP8X4),
                    rhs_scale=wscales[:],
                    start=True,
                    stop=True,
                )
                st[("acc" + tag, g, j)] = acc

        def c(g, j):
            if j == 0:
                st[("sums", g)] = small.tile([P, 2], F32, name="sums", tag="sums")
            u_t = work.tile([P, D], F32, name="u_t", tag="u", bufs=10)
            nc.vector.scalar_tensor_tensor(
                out=u_t[:],
                in0=st[("acc1", g, j)][:],
                scalar=0.2,
                in1=hid[g][:, D * j : D * (j + 1)],
                op0=ALU.mult,
                op1=ALU.add,
                accum_out=st[("sums", g)][:, j : j + 1],
            )
            st[("u", g, j)] = u_t

        def nm(g):
            negmean = small.tile([P, 2], F32, name="negmean", tag="negmean")
            nc.scalar.mul(out=negmean[:], in_=st[("sums", g)][:], mul=-1.0 / D)
            st[("negmean", g)] = negmean

        def d(g, j):
            if j == 0:
                st[("ssq", g)] = small.tile([P, 2], F32, name="ssq", tag="ssq")
            junk = work.tile([P, D], BF16, name="junk", tag="junk")
            nc.scalar.activation(
                out=junk[:],
                in_=st[("u", g, j)][:],
                func=ACT.Square,
                bias=st[("sums", g)][:, j : j + 1],
                scale=-float(D),
                accum_out=st[("ssq", g)][:, j : j + 1],
            )

        def rs(g):
            std = small.tile([P, 2], F32, name="std", tag="std")
            nc.scalar.activation(out=std[:], in_=st[("ssq", g)][:], func=ACT.Sqrt, bias=eps_t[:], scale=1.0 / D**3)
            st[("std", g)] = std

        def rc(g):
            rstd = small.tile([P, 2], F32, name="rstd", tag="rstd")
            nc.vector.reciprocal(out=rstd[:], in_=st[("std", g)][:])
            st[("rstd", g)] = rstd

        def z(g, j, engine=nc.gpsimd):
            z_t = work.tile([P, D], F32, name="z_t", tag="z", bufs=8)
            engine.tensor_scalar(
                out=z_t[:],
                in0=st[("u", g, j)][:],
                scalar1=st[("negmean", g)][:, j : j + 1],
                scalar2=st[("rstd", g)][:, j : j + 1],
                op0=ALU.add,
                op1=ALU.mult,
            )
            st[("z", g, j)] = z_t

        def t2(g, half, bank=None):
            bank = bank or "zT%d" % half
            z_ps = psum.tile([P, 2, 2 * P], F32, name="z_ps", tag=bank, bufs=2 if bank == "acc1" else 1)
            for t2i in range(2):
                t = 2 * half + t2i
                for j in range(2):
                    nc.tensor.transpose(
                        z_ps[:, t2i, P * j : P * (j + 1)], st[("z", g, j)][:, P * t : P * (t + 1)], ident_f[:]
                    )
            st[("z_ps", g, half)] = z_ps

        def f1(g, half):
            if half == 0:
                st[("hn_t", g)] = work.tile([P, 4, 2 * P], F32, name="hn_t", tag="hn_t", bufs=4)
            for t2i in range(2):
                t = 2 * half + t2i
                nc.scalar.activation(
                    out=st[("hn_t", g)][:, t, :],
                    in_=st[("z_ps", g, half)][:, t2i, :],
                    func=ACT.Identity,
                    bias=bet_t[:, t : t + 1],
                    scale=gam_t[:, t : t + 1],
                )

        def r(g, engine=nc.gpsimd):
            g2 = work.tile([P, 2 * D], BF16, name="g2", tag="g2", align_bytes=64, bufs=4)
            engine.tensor_scalar(
                out=g2[:].rearrange("p (c i t) -> p c t i", i=4, t=4),
                in0=st[("hn_t", g)][:].rearrange("p t (c i) -> p c t i", i=4),
                scalar1=1.0,
                scalar2=0.0,
                op0=ALU.mult,
                op1=ALU.add,
            )
            st[("g2", g)] = g2

        def t3(g, j, bank="hB"):
            h_ps = psum.tile([P, D], F32, name="h_ps", tag=bank, bufs=2 if bank == "acc1" else 1)
            for t in range(4):
                nc.tensor.transpose(
                    h_ps[:, P * t : P * (t + 1)], st[("hn_t", g)][:, t, P * j : P * (j + 1)], ident_f[:]
                )
            st[("h_ps", g, j)] = h_ps

        def o(g, j):
            if j == 0:
                st[("hn", g)] = work.tile([P, 2, D], F32, name="hn", tag="hn", bufs=4)
            nc.scalar.copy(out=st[("hn", g)][:, j, :], in_=st[("h_ps", g, j)][:])
            if g >= PAIRS - 3:
                nc.sync.dma_start(out=out0_v[g][:, j], in_=st[("hn", g)][:, j])
            elif j == 1:
                nc.sync.dma_start(out=out0_v[g], in_=st[("hn", g)][:])

        def h(g, j):
            if j == 0:
                st[("pred", g)] = work.tile([P, 2, D], F32, name="pred", tag="pred", bufs=4)
            nc.vector.tensor_tensor(
                out=st[("pred", g)][:, j, :], in0=st[("acc2", g, j)][:], in1=bg_b[:], op=ALU.add
            )
            if g >= PAIRS - 3:
                nc.sync.dma_start(out=out1_v[g][:, j], in_=st[("pred", g)][:, j])
            elif j == 1:
                nc.sync.dma_start(out=out1_v[g], in_=st[("pred", g)][:])

        def run(stage, g, *args):
            if 0 <= g < PAIRS:
                stage(g, *args)

        t1(0)
        a(0)
        t1(1)
        nc.vector.quantize_mx(
            out=w1codes[:].bitcast(FP8X4), scales=w1sc[:], in_=w1grp[:].rearrange("p n t -> p (n t)")
        )
        quantise(0, "g1", "1")
        mx(0, "1", w1codes, w1sc)
        a(1)
        t1(2)
        w2_transposes(0)
        w2_transposes(1)
        for f in range(PAIRS):
            run(d, f - 1, 0)
            run(t2, f - 2, 1)
            run(d, f - 1, 1)
            if 1 <= f and f not in (2, 3):
                run(mx, f, "1", w1codes, w1sc)
            run(rs, f - 1)
            run(nm, f - 1)
            if f == 1:
                w2_copy(nc.scalar.copy, 0)
                w2_copy(nc.scalar.copy, 1)
            run(r, f - 3)
            if f >= 1:
                run(t1, f + 2)
            if f in (0,):
                run(c, f, 0)
                run(c, f, 1)
            run(rc, f - 1)
            run(quantise, f - 3, "g2", "2")
            run(quantise, f + 1, "g1", "1")
            if f == 2:
                w2_quantise()
            run(z, f - 1, 1)
            run(o, f - 3, 0)
            run(t3, f - 3, 1)
            run(f1, f - 2, 0)
            run(mx, f - 3, "2", w2codes, w2sc)
            run(z, f - 1, 0)
            if f not in (0,):
                run(c, f, 0)
                run(c, f, 1)
            run(h, f - 3, 0)
            run(h, f - 3, 1)
            run(a, f + 2)
            run(f1, f - 2, 1)
            run(o, f - 3, 1)
            if f + 1 in (2, 3):
                run(mx, f + 1, "1", w1codes, w1sc)
            run(t2, f - 1, 0)
            run(t3, f - 2, 0)
        y, x, w, v = PAIRS - 1, PAIRS - 2, PAIRS - 3, PAIRS - 4
        d(y, 0)
        d(y, 1)
        t2(x, 1)
        t3(w, 1, "acc1")
        o(w, 0)
        rs(y)
        nm(y)
        r(w)
        quantise(w, "g2", "2")
        mx(w, "2", w2codes, w2sc)
        f1(x, 0)
        f1(x, 1)
        rc(y)
        z(y, 0, nc.vector)
        z(y, 1, nc.vector)
        t2(y, 0, "xt")
        t2(y, 1, "acc1")
        o(w, 1)
        h(w, 0)
        h(w, 1)
        f1(y, 0)
        f1(y, 1)
        t3(x, 0)
        t3(x, 1, "acc1")
        r(x, nc.vector)
        quantise(x, "g2", "2")
        mx(x, "2", w2codes, w2sc)
        r(y, nc.vector)
        o(x, 0)
        o(x, 1)
        h(x, 0)
        quantise(y, "g2", "2")
        t3(y, 0, "zT0")
        t3(y, 1, "zT1")
        h(x, 1)
        mx(y, "2", w2codes, w2sc)
        o(y, 0)
        o(y, 1)
        h(y, 0)
        h(y, 1)
